import numpy as np
import ml_dtypes


def mxq(x, axis, fmt="e4m3"):
    dtype, down = {"e4m3": (ml_dtypes.float8_e4m3fn, 7), "e5m2": (ml_dtypes.float8_e5m2, 14)}[fmt]
    v = np.moveaxis(np.asarray(x, np.float32).astype(ml_dtypes.bfloat16).astype(np.float64), axis, -1)
    blocks = v.reshape(v.shape[:-1] + (-1, 32))
    amax = np.abs(blocks).max(-1, keepdims=True)
    byte = np.maximum(np.where(amax > 0, np.frexp(amax)[1] - 1 + 127, 0) - down, 1)
    scale = np.exp2(byte - 127.0)
    codes = (blocks / scale).astype(np.float32).astype(dtype).astype(np.float64)
    return np.moveaxis((codes * scale).reshape(v.shape), -1, axis)


WIDE = False


def mx_kscale(k):
    if not WIDE:
        return np.ones(k)
    levels = np.array([10, -10, 5, -5, 0])
    if k % 512:
        return np.exp2(np.random.permutation(np.resize(levels, k // 32))).repeat(32)
    a = np.empty((k // 512, 16))
    for p in range(k // 512):
        a[p, :8] = np.random.permutation(np.resize(levels, 8))
        for g in range(8):
            far = levels[np.abs(levels - a[p, g]) >= 10]
            a[p, g + 8] = far[np.random.randint(len(far))]
    return np.exp2(a.ravel()).repeat(32)


BF16 = ml_dtypes.bfloat16


def bf(x):
    return np.asarray(x, np.float32).astype(BF16)


def f64(x):
    return np.asarray(x).astype(np.float64)


B, S, D, BD, K = 8, 1024, 512, 512, 128
TS = 3.0


def sigmoid(v):
    return 1.0 / (1.0 + np.exp(-v))


def setup_inputs():
    s = mx_kscale(D)
    return {
        "token_embeddings": bf(np.random.standard_normal((B, S, D)) * TS * s),
        "splat_influences": bf(np.random.uniform(size=(B, S, K))),
        "decoded": bf(np.random.standard_normal((B, K, D)) * 0.35),
        "gate_W": bf(np.random.standard_normal((D, D)) / (TS * np.sqrt(D)) / s[:, None]),
        "gate_b": bf(np.random.standard_normal(D) * 0.5),
    }


def reference(token_embeddings, splat_influences, decoded, gate_W, gate_b):
    flow = f64(splat_influences) @ f64(decoded)
    gate = sigmoid((mxq(f64(token_embeddings), 2, "e4m3") @ mxq(f64(gate_W), 0, "e4m3")) + f64(gate_b))
    return flow * gate

@@ -1,0 +1,255 @@
+from contextlib import ExitStack
+
+import concourse.mybir as mybir
+from concourse.masks import make_identity
+
+F32 = mybir.dt.float32
+BF16 = mybir.dt.bfloat16
+U32 = mybir.dt.uint32
+U8 = mybir.dt.uint8
+FP8X4 = mybir.dt.float8_e4m3fn_x4
+ADD = mybir.AluOpType.add
+MULT = mybir.AluOpType.mult
+SIGMOID = mybir.ActivationFunctionType.Sigmoid
+
+P = 128
+BATCH, TOKENS, FEAT, SPLATS = 8, 1024, 512, 128
+SLOTS = TOKENS // P
+N_TILES = BATCH * SLOTS
+N_PAIRS = N_TILES // 2
+STORE = 4
+FLOPS = 2 * BATCH * TOKENS * FEAT * FEAT + 2 * BATCH * TOKENS * SPLATS * FEAT
+
+POOL_TILES = (3, 7, 11, 15, 5, 13)
+POOL_TAIL = (56, 58)
+CHUNKS = 2
+
+
+def tile_splatinformationflow_pb_t_kernel(
+    tc, token_embeddings, splat_influences, decoded, gate_W, gate_b, out
+):
+    nc = tc.nc
+    x_dram = token_embeddings.rearrange("b (p j) k -> b p (j k)", j=SLOTS)
+    i_dram = splat_influences.rearrange("b (p j) s -> p b (j s)", j=SLOTS)
+    d_dram = decoded.rearrange("b s d -> s b d")
+    o_dram = out.rearrange("b (p j) d -> b p (j d)", j=SLOTS)
+
+    with ExitStack() as ctx:
+        ctx.enter_context(tc.manual_schedule())
+        const = ctx.enter_context(tc.tile_pool(name="const", bufs=1))
+        stage = ctx.enter_context(tc.tile_pool(name="stage", bufs=3))
+        zpool = ctx.enter_context(tc.tile_pool(name="zpool", bufs=6))
+        fpool = ctx.enter_context(tc.tile_pool(name="fpool", bufs=3))
+        opool = ctx.enter_context(tc.tile_pool(name="opool", bufs=6))
+        ps_t = ctx.enter_context(tc.psum_pool(name="ps_t", bufs=2))
+        ps_g = ctx.enter_context(tc.psum_pool(name="ps_g", bufs=3))
+        ps_f = ctx.enter_context(tc.psum_pool(name="ps_f", bufs=3))
+
+        x_sb = [const.tile([P, SLOTS * FEAT], BF16, name="x%d" % b) for b in range(BATCH)]
+        i_a = const.tile([P, 1, SLOTS * SPLATS], BF16)
+        i_b = const.tile([P, 3, SLOTS * SPLATS], BF16)
+        i_c = const.tile([P, 4, SLOTS * SPLATS], BF16)
+        d_a = const.tile([P, 1, FEAT], BF16)
+        d_b = const.tile([P, 7, FEAT], BF16)
+        w_raw = const.tile([P, 4, FEAT], BF16)
+        w_grp = const.tile([P, FEAT, 4], BF16, align_bytes=64)
+        w_codes = const.tile([P, FEAT], U32, align_bytes=64)
+        w_scales = const.tile([P, FEAT], U8, align_bytes=64)
+        b_row = const.tile([P, FEAT], BF16)
+        ones = const.tile([P, P], BF16)
+        bias = const.tile([P, FEAT], F32)
+        ident_f = const.tile([P, P], F32)
+        ident_b = const.tile([P, P], BF16)
+        warm = const.tile([P, 1], F32)
+
+        def infl(b):
+            if b == 0:
+                return i_a[:, 0, :]
+            if b < 4:
+                return i_b[:, b - 1, :]
+            return i_c[:, b - 4, :]
+
+        def dec(b):
+            return d_a[:, 0, :] if b == 0 else d_b[:, b - 1, :]
+
+        nc.vector.memset(warm[:], 0.0)
+        nc.vector.memset(b_row[:], 0.0)
+        nc.vector.memset(ones[:], 1.0)
+        nc.scalar.activation(out=warm[:], in_=warm[:], func=SIGMOID)
+        make_identity(nc, ident_f[:])
+        make_identity(nc, ident_b[:])
+
+        quarter = SLOTS * FEAT // 4
+        nc.sync.dma_start(
+            out=w_raw[:],
+            in_=gate_W.rearrange("(q t) n -> q t n", t=4),
+        )
+        nc.sync.dma_start(out=b_row[0:1, :], in_=gate_b.rearrange("(o n) -> o n", o=1))
+        nc.sync.dma_start(out=x_sb[0][:, 0:quarter], in_=x_dram[0][:, 0:quarter])
+        nc.sync.dma_start(out=x_sb[0][:, quarter : 2 * quarter], in_=x_dram[0][:, quarter : 2 * quarter])
+        nc.sync.dma_start(out=x_sb[0][:, 2 * quarter :], in_=x_dram[0][:, 2 * quarter :])
+        nc.sync.dma_start(out=i_a[:], in_=i_dram[:, 0:1, :])
+        nc.sync.dma_start(out=d_a[:], in_=d_dram[:, 0:1, :])
+        nc.sync.dma_start(out=x_sb[1][:], in_=x_dram[1])
+        nc.sync.dma_start(out=i_b[:], in_=i_dram[:, 1:4, :])
+        nc.sync.dma_start(out=d_b[:], in_=d_dram[:, 1:8, :])
+        nc.sync.dma_start(out=x_sb[2][:], in_=x_dram[2])
+        nc.sync.dma_start(out=x_sb[3][:], in_=x_dram[3])
+        nc.sync.dma_start(out=i_c[:], in_=i_dram[:, 4:8, :])
+        for b in range(4, BATCH):
+            nc.sync.dma_start(out=x_sb[b][:], in_=x_dram[b])
+
+        xts, its, grps, codes, planes, infl_t, gs, fs, f_sbs, zs, o_sbs = {}, {}, {}, {}, {}, {}, {}, {}, {}, {}, {}
+
+        def weights():
+            nc.vector.tensor_copy(out=w_grp[:], in_=w_raw[:].rearrange("p t n -> p n t"))
+            nc.vector.quantize_mx(
+                out=w_codes[:].bitcast(FP8X4), scales=w_scales[:], in_=w_grp[:].rearrange("p n t -> p (n t)")
+            )
+
+        def bias_rows():
+            b_ps = ps_f.tile([P, FEAT], F32, tag="f_ps")
+            fs["bias"] = b_ps
+            nc.tensor.matmul(out=b_ps[:], lhsT=ones[:], rhs=b_row[:], start=True, stop=True)
+
+        def t_x(q):
+            words = x_sb[q // 4][:].bitcast(F32)
+            xt = ps_t.tile([P, 2, 2, P], F32, tag="t")
+            xts[q] = xt
+            for s in range(2):
+                for u in range(2):
+                    w0 = (2 * (q % 4) + s) * (FEAT // 2)
+                    nc.tensor.transpose(xt[:, s, u, :], words[:, w0 + u : w0 + 2 * P : 2], ident_f[:])
+
+        def t_i(b):
+            it = ps_t.tile([P, SLOTS, P], BF16, tag="t")
+            its[b] = it
+            for j in range(SLOTS):
+                nc.tensor.transpose(it[:, j, :], infl(b)[:, j * SPLATS : (j + 1) * SPLATS], ident_b[:])
+
+        def c_x(q):
+            if q % 2 == 0:
+                grp = stage.tile([P, 4 * P * 4], BF16, align_bytes=64)
+                grps[q // 2] = grp
+            dst = grps[q // 2][:].bitcast(F32).rearrange("p (s r u) -> p s r u", s=4, u=2)
+            a = 2 * (q % 2)
+            nc.scalar.copy(out=dst[:, a : a + 2], in_=xts[q][:].rearrange("p s u r -> p s r u"))
+
+        def c_i(b):
+            i_t = stage.tile([P, SLOTS, P], BF16, bufs=2)
+            infl_t[b] = i_t
+            nc.scalar.copy(out=i_t[:], in_=its[b][:])
+
+        def quantise(g, first, count):
+            if first == 0:
+                cod = stage.tile([P, 4 * P], U32, align_bytes=64)
+                pla = stage.tile([P, 4 * P], U8, align_bytes=64)
+                codes[g], planes[g] = cod, pla
+            cols = slice(first * P, (first + count) * P)
+            nc.vector.quantize_mx(
+                out=codes[g][:, cols].bitcast(FP8X4),
+                scales=planes[g][:, cols],
+                in_=grps[g][:, 4 * first * P : 4 * (first + count) * P],
+            )
+
+        def mx(n):
+            cols = slice((n % 4) * P, (n % 4 + 1) * P)
+            g_ps = ps_g.tile([P, FEAT], F32)
+            gs[n] = g_ps
+            nc.tensor.matmul_mx(
+                out=g_ps[:],
+                lhsT=codes[n // 4][:, cols].bitcast(FP8X4),
+                lhsT_scale=planes[n // 4][:, cols],
+                rhs=w_codes[:].bitcast(FP8X4),
+                rhs_scale=w_scales[:],
+                start=True,
+                stop=True,
+            )
+
+        def plain(n):
+            f_ps = ps_f.tile([P, FEAT], F32)
+            fs[n] = f_ps
+            nc.tensor.matmul(
+                out=f_ps[:], lhsT=infl_t[n // SLOTS][:, n % SLOTS, :], rhs=dec(n // SLOTS), start=True, stop=True
+            )
+
+        def add_bias(n):
+            z = zpool.tile([P, FEAT], F32)
+            zs[n] = z
+            nc.vector.tensor_tensor(out=z[:], in0=gs[n][:], in1=bias[:], op=ADD)
+
+        def sigmoid(n):
+            nc.scalar.activation(out=zs[n][:], in_=zs[n][:], func=SIGMOID)
+
+        def by_pool(n):
+            return (n % 16 in POOL_TILES and n < 56) or n in POOL_TAIL
+
+        def flow_copy(n):
+            f_sb = fpool.tile([P, FEAT], F32)
+            f_sbs[n] = f_sb
+            nc.scalar.copy(out=f_sb[:], in_=fs[n][:])
+
+        def product(n):
+            g, c = n // STORE, n % STORE
+            if c == 0:
+                o = opool.tile([P, STORE, FEAT], F32)
+                o_sbs[g] = o
+            if by_pool(n):
+                w = FEAT // CHUNKS
+                for i in range(CHUNKS):
+                    cs = slice(i * w, (i + 1) * w)
+                    nc.gpsimd.tensor_tensor(out=o_sbs[g][:, c, cs], in0=f_sbs[n][:, cs], in1=zs[n][:, cs], op=MULT)
+            else:
+                nc.vector.tensor_tensor(out=o_sbs[g][:, c, :], in0=fs[n][:], in1=zs[n][:], op=MULT)
+
+        def store(n0, n1):
+            b, g = n0 // SLOTS, n0 // STORE
+            nc.sync.dma_start(
+                out=o_dram[b][:, (n0 % SLOTS) * FEAT : (n0 % SLOTS + n1 - n0) * FEAT],
+                in_=o_sbs[g][:, n0 % STORE : n0 % STORE + n1 - n0, :].rearrange("p c d -> p (c d)"),
+            )
+
+        def tile_ok(n):
+            return 0 <= n < N_TILES
+
+        for n in range(-9, N_TILES + 1):
+            if tile_ok(n + 4):
+                mx(n + 4)
+            if tile_ok(n + 2):
+                plain(n + 2)
+            if (n + 9) % 2 == 0 and 0 <= (n + 9) // 2 < N_PAIRS:
+                t_x((n + 9) // 2)
+            if n == -9:
+                bias_rows()
+            if n == -4:
+                t_i(0)
+            if (n + 8) % 8 == 0 and 1 <= (n + 8) // 8 < BATCH:
+                t_i((n + 8) // 8)
+            if tile_ok(n + 1):
+                sigmoid(n + 1)
+            if (n + 8) % 2 == 0 and 0 <= (n + 8) // 2 < N_PAIRS:
+                c_x((n + 8) // 2)
+            if n == -3:
+                c_i(0)
+            if (n + 7) % 8 == 0 and 1 <= (n + 7) // 8 < BATCH:
+                c_i((n + 7) // 8)
+            if tile_ok(n) and by_pool(n):
+                flow_copy(n)
+            if n == -8:
+                weights()
+            if tile_ok(n + 2):
+                add_bias(n + 2)
+            if n == -7:
+                quantise(0, 0, 2)
+            if n == -6:
+                nc.vector.tensor_copy(out=bias[:], in_=fs["bias"][:])
+            if n == -5:
+                quantise(0, 2, 2)
+            if (n + 5) % 4 == 0 and 1 <= (n + 5) // 4 < N_TILES // 4:
+                quantise((n + 5) // 4, 0, 4)
+            if tile_ok(n):
+                product(n)
+            if tile_ok(n - 1) and (n - 1) % 2 == 1 and n - 1 < N_TILES - STORE:
+                store(n - 2, n)
+            if n >= N_TILES - STORE and tile_ok(n):
+                store(n, n + 1)

@@ -79,32 +79,39 @@ def tile_splatinformationflow_pb_t_kernel(
         make_identity(nc, ident_f[:])
         make_identity(nc, ident_b[:])
 
-        quarter = SLOTS * FEAT // 4
-        nc.sync.dma_start(
-            out=w_raw[:],
-            in_=gate_W.rearrange("(q t) n -> q t n", t=4),
-        )
+        def load_x(b, j0, j1):
+            cols = slice(j0 * FEAT, j1 * FEAT)
+            nc.sync.dma_start(out=x_sb[b][:, cols], in_=x_dram[b][:, cols])
+
+        load_x(0, 0, 1)
+        nc.sync.dma_start(out=w_raw[:], in_=gate_W.rearrange("(q t) n -> q t n", t=4))
+        load_x(0, 1, 2)
         nc.sync.dma_start(out=b_row[0:1, :], in_=gate_b.rearrange("(o n) -> o n", o=1))
-        nc.sync.dma_start(out=x_sb[0][:, 0:quarter], in_=x_dram[0][:, 0:quarter])
-        nc.sync.dma_start(out=x_sb[0][:, quarter : 2 * quarter], in_=x_dram[0][:, quarter : 2 * quarter])
-        nc.sync.dma_start(out=x_sb[0][:, 2 * quarter :], in_=x_dram[0][:, 2 * quarter :])
+        load_x(0, 2, 4)
         nc.sync.dma_start(out=i_a[:], in_=i_dram[:, 0:1, :])
+        load_x(0, 4, 6)
         nc.sync.dma_start(out=d_a[:], in_=d_dram[:, 0:1, :])
-        nc.sync.dma_start(out=x_sb[1][:], in_=x_dram[1])
+        load_x(0, 6, 8)
+        load_x(1, 0, 4)
+        load_x(1, 4, 8)
         nc.sync.dma_start(out=i_b[:], in_=i_dram[:, 1:4, :])
         nc.sync.dma_start(out=d_b[:], in_=d_dram[:, 1:8, :])
-        nc.sync.dma_start(out=x_sb[2][:], in_=x_dram[2])
-        nc.sync.dma_start(out=x_sb[3][:], in_=x_dram[3])
+        load_x(2, 0, 8)
+        load_x(3, 0, 8)
         nc.sync.dma_start(out=i_c[:], in_=i_dram[:, 4:8, :])
         for b in range(4, BATCH):
-            nc.sync.dma_start(out=x_sb[b][:], in_=x_dram[b])
+            load_x(b, 0, 8)
 
         xts, its, grps, codes, planes, infl_t, gs, fs, f_sbs, zs, o_sbs = {}, {}, {}, {}, {}, {}, {}, {}, {}, {}, {}
 
-        def weights():
-            nc.vector.tensor_copy(out=w_grp[:], in_=w_raw[:].rearrange("p t n -> p n t"))
+        def w_copy(copy, c0, c1):
+            copy(out=w_grp[:, c0:c1, :], in_=w_raw[:, :, c0:c1].rearrange("p t n -> p n t"))
+
+        def w_quantise(c0, c1):
             nc.vector.quantize_mx(
-                out=w_codes[:].bitcast(FP8X4), scales=w_scales[:], in_=w_grp[:].rearrange("p n t -> p (n t)")
+                out=w_codes[:, c0:c1].bitcast(FP8X4),
+                scales=w_scales[:, c0:c1],
+                in_=w_grp[:, c0:c1, :].rearrange("p n t -> p (n t)"),
             )
 
         def bias_rows():
@@ -112,11 +119,13 @@ def tile_splatinformationflow_pb_t_kernel(
             fs["bias"] = b_ps
             nc.tensor.matmul(out=b_ps[:], lhsT=ones[:], rhs=b_row[:], start=True, stop=True)
 
-        def t_x(q):
+        def t_x(q, s0, s1):
             words = x_sb[q // 4][:].bitcast(F32)
-            xt = ps_t.tile([P, 2, 2, P], F32, tag="t")
-            xts[q] = xt
-            for s in range(2):
+            if s0 == 0:
+                xt = ps_t.tile([P, 2, 2, P], F32, tag="t")
+                xts[q] = xt
+            xt = xts[q]
+            for s in range(s0, s1):
                 for u in range(2):
                     w0 = (2 * (q % 4) + s) * (FEAT // 2)
                     nc.tensor.transpose(xt[:, s, u, :], words[:, w0 + u : w0 + 2 * P : 2], ident_f[:])
@@ -127,13 +136,13 @@ def tile_splatinformationflow_pb_t_kernel(
             for j in range(SLOTS):
                 nc.tensor.transpose(it[:, j, :], infl(b)[:, j * SPLATS : (j + 1) * SPLATS], ident_b[:])
 
-        def c_x(q):
-            if q % 2 == 0:
+        def c_x(q, s0, s1):
+            if q % 2 == 0 and s0 == 0:
                 grp = stage.tile([P, 4 * P * 4], BF16, align_bytes=64)
                 grps[q // 2] = grp
             dst = grps[q // 2][:].bitcast(F32).rearrange("p (s r u) -> p s r u", s=4, u=2)
             a = 2 * (q % 2)
-            nc.scalar.copy(out=dst[:, a : a + 2], in_=xts[q][:].rearrange("p s u r -> p s r u"))
+            nc.scalar.copy(out=dst[:, a + s0 : a + s1], in_=xts[q][:, s0:s1].rearrange("p s u r -> p s r u"))
 
         def c_i(b):
             i_t = stage.tile([P, SLOTS, P], BF16, bufs=2)
@@ -167,7 +176,7 @@ def tile_splatinformationflow_pb_t_kernel(
             )
 
         def plain(n):
-            f_ps = ps_f.tile([P, FEAT], F32)
+            f_ps = ps_f.tile([P, FEAT], F32, tag="f_ps")
             fs[n] = f_ps
             nc.tensor.matmul(
                 out=f_ps[:], lhsT=infl_t[n // SLOTS][:, n % SLOTS, :], rhs=dec(n // SLOTS), start=True, stop=True
@@ -202,6 +211,9 @@ def tile_splatinformationflow_pb_t_kernel(
             else:
                 nc.vector.tensor_tensor(out=o_sbs[g][:, c, :], in0=fs[n][:], in1=zs[n][:], op=MULT)
 
+        def bias_copy():
+            nc.vector.tensor_copy(out=bias[:], in_=fs["bias"][:])
+
         def store(n0, n1):
             b, g = n0 // SLOTS, n0 // STORE
             nc.sync.dma_start(
@@ -209,47 +221,42 @@ def tile_splatinformationflow_pb_t_kernel(
                 in_=o_sbs[g][:, n0 % STORE : n0 % STORE + n1 - n0, :].rearrange("p c d -> p (c d)"),
             )
 
-        def tile_ok(n):
-            return 0 <= n < N_TILES
+        calls = []
 
-        for n in range(-9, N_TILES + 1):
-            if tile_ok(n + 4):
-                mx(n + 4)
-            if tile_ok(n + 2):
-                plain(n + 2)
-            if (n + 9) % 2 == 0 and 0 <= (n + 9) // 2 < N_PAIRS:
-                t_x((n + 9) // 2)
-            if n == -9:
-                bias_rows()
-            if n == -4:
-                t_i(0)
-            if (n + 8) % 8 == 0 and 1 <= (n + 8) // 8 < BATCH:
-                t_i((n + 8) // 8)
-            if tile_ok(n + 1):
-                sigmoid(n + 1)
-            if (n + 8) % 2 == 0 and 0 <= (n + 8) // 2 < N_PAIRS:
-                c_x((n + 8) // 2)
-            if n == -3:
-                c_i(0)
-            if (n + 7) % 8 == 0 and 1 <= (n + 7) // 8 < BATCH:
-                c_i((n + 7) // 8)
-            if tile_ok(n) and by_pool(n):
-                flow_copy(n)
-            if n == -8:
-                weights()
-            if tile_ok(n + 2):
-                add_bias(n + 2)
-            if n == -7:
-                quantise(0, 0, 2)
-            if n == -6:
-                nc.vector.tensor_copy(out=bias[:], in_=fs["bias"][:])
-            if n == -5:
-                quantise(0, 2, 2)
-            if (n + 5) % 4 == 0 and 1 <= (n + 5) // 4 < N_TILES // 4:
-                quantise((n + 5) // 4, 0, 4)
-            if tile_ok(n):
-                product(n)
-            if tile_ok(n - 1) and (n - 1) % 2 == 1 and n - 1 < N_TILES - STORE:
-                store(n - 2, n)
-            if n >= N_TILES - STORE and tile_ok(n):
-                store(n, n + 1)
+        def at(when, call, *args):
+            calls.append((when, call, args))
+
+        at(-11.5, w_copy, nc.scalar.copy, 384, 512)
+        at(-11.5, w_copy, nc.vector.tensor_copy, 0, 256)
+        at(-11.5, w_copy, nc.vector.tensor_copy, 256, 384)
+        at(-7, w_quantise, 0, 256)
+        at(-5.9, w_quantise, 256, 512)
+        at(-7.5, bias_rows)
+        at(-6.5, bias_copy)
+        for s in range(2):
+            at(-11.4 + s * 0.1, t_x, 0, s, s + 1)
+            at(-10 + s * 0.1, c_x, 0, s, s + 1)
+        at(-6.45 + -2, quantise, 0, 0, 2)
+        at(-6.45 + 2, quantise, 0, 2, 2)
+        for q in range(1, N_PAIRS):
+            at(2 * (q - q % 1) - 11.4 + 0.01 * (q % 1), t_x, q, 0, 2)
+            at(2 * q - 10, c_x, q, 0, 2)
+        for g in range(1, N_TILES // 4):
+            at(4 * g - 6.45, quantise, g, 0, 4)
+        for b in range(BATCH):
+            at(8 * b - 8.8 + (0 if b == 0 else 0), t_i, b)
+            at(8 * b - 7 + (0 if b == 0 else 0), c_i, b)
+        for n in range(N_TILES):
+            at(n - 3.5, mx, n)
+            at(n - 1.4, plain, n)
+            at(n - 2.3, add_bias, n)
+            at(n - 0.4, sigmoid, n)
+            if by_pool(n):
+                at(n - 0.1, flow_copy, n)
+            at(n + (0 if by_pool(n) else 0), product, n)
+            if n >= N_TILES - STORE:
+                at(n + 0.05, store, n, n + 1)
+            elif n % 2 == 1:
+                at(n + 1.05, store, n - 1, n + 1)
+        for when, call, args in sorted(calls, key=lambda c: c[0]):
+            call(*args)

@@ -23,6 +23,7 @@ FLOPS = 2 * BATCH * TOKENS * FEAT * FEAT + 2 * BATCH * TOKENS * SPLATS * FEAT
 POOL_TILES = (3, 7, 11, 15, 5, 13)
 POOL_TAIL = (56, 58)
 CHUNKS = 2
+RUN = 1
 
 
 def tile_splatinformationflow_pb_t_kernel(
@@ -46,11 +47,8 @@ def tile_splatinformationflow_pb_t_kernel(
         ps_f = ctx.enter_context(tc.psum_pool(name="ps_f", bufs=3))
 
         x_sb = [const.tile([P, SLOTS * FEAT], BF16, name="x%d" % b) for b in range(BATCH)]
-        i_a = const.tile([P, 1, SLOTS * SPLATS], BF16)
-        i_b = const.tile([P, 3, SLOTS * SPLATS], BF16)
-        i_c = const.tile([P, 4, SLOTS * SPLATS], BF16)
-        d_a = const.tile([P, 1, FEAT], BF16)
-        d_b = const.tile([P, 7, FEAT], BF16)
+        i_sb = const.tile([P, BATCH, SLOTS * SPLATS], BF16)
+        d_sb = const.tile([P, BATCH, FEAT], BF16)
         w_raw = const.tile([P, 4, FEAT], BF16)
         w_grp = const.tile([P, FEAT, 4], BF16, align_bytes=64)
         w_codes = const.tile([P, FEAT], U32, align_bytes=64)
@@ -61,16 +59,6 @@ def tile_splatinformationflow_pb_t_kernel(
         ident_f = const.tile([P, P], F32)
         ident_b = const.tile([P, P], BF16)
         warm = const.tile([P, 1], F32)
-
-        def infl(b):
-            if b == 0:
-                return i_a[:, 0, :]
-            if b < 4:
-                return i_b[:, b - 1, :]
-            return i_c[:, b - 4, :]
-
-        def dec(b):
-            return d_a[:, 0, :] if b == 0 else d_b[:, b - 1, :]
 
         nc.vector.memset(warm[:], 0.0)
         nc.vector.memset(b_row[:], 0.0)
@@ -83,26 +71,27 @@ def tile_splatinformationflow_pb_t_kernel(
             cols = slice(j0 * FEAT, j1 * FEAT)
             nc.sync.dma_start(out=x_sb[b][:, cols], in_=x_dram[b][:, cols])
 
-        load_x(0, 0, 1)
         nc.sync.dma_start(out=w_raw[:], in_=gate_W.rearrange("(q t) n -> q t n", t=4))
-        load_x(0, 1, 2)
         nc.sync.dma_start(out=b_row[0:1, :], in_=gate_b.rearrange("(o n) -> o n", o=1))
+        load_x(0, 0, 1)
+        load_x(0, 1, 2)
         load_x(0, 2, 4)
-        nc.sync.dma_start(out=i_a[:], in_=i_dram[:, 0:1, :])
+        nc.sync.dma_start(out=i_sb[:, 0:1, :], in_=i_dram[:, 0:1, :])
         load_x(0, 4, 6)
-        nc.sync.dma_start(out=d_a[:], in_=d_dram[:, 0:1, :])
+        nc.sync.dma_start(out=d_sb[:, 0:1, :], in_=d_dram[:, 0:1, :])
         load_x(0, 6, 8)
         load_x(1, 0, 4)
         load_x(1, 4, 8)
-        nc.sync.dma_start(out=i_b[:], in_=i_dram[:, 1:4, :])
-        nc.sync.dma_start(out=d_b[:], in_=d_dram[:, 1:8, :])
+        nc.sync.dma_start(out=i_sb[:, 1:2, :], in_=i_dram[:, 1:2, :])
+        nc.sync.dma_start(out=d_sb[:, 1:8, :], in_=d_dram[:, 1:8, :])
+        nc.sync.dma_start(out=i_sb[:, 2:4, :], in_=i_dram[:, 2:4, :])
         load_x(2, 0, 8)
         load_x(3, 0, 8)
-        nc.sync.dma_start(out=i_c[:], in_=i_dram[:, 4:8, :])
+        nc.sync.dma_start(out=i_sb[:, 4:8, :], in_=i_dram[:, 4:8, :])
         for b in range(4, BATCH):
             load_x(b, 0, 8)
 
-        xts, its, grps, codes, planes, infl_t, gs, fs, f_sbs, zs, o_sbs = {}, {}, {}, {}, {}, {}, {}, {}, {}, {}, {}
+        xts, its, grps, codes, planes, infl_t, gs, fs, f_sbs, zs, z_tiles, o_sbs = {}, {}, {}, {}, {}, {}, {}, {}, {}, {}, {}, {}
 
         def w_copy(copy, c0, c1):
             copy(out=w_grp[:, c0:c1, :], in_=w_raw[:, :, c0:c1].rearrange("p t n -> p n t"))
@@ -130,11 +119,16 @@ def tile_splatinformationflow_pb_t_kernel(
                     w0 = (2 * (q % 4) + s) * (FEAT // 2)
                     nc.tensor.transpose(xt[:, s, u, :], words[:, w0 + u : w0 + 2 * P : 2], ident_f[:])
 
-        def t_i(b):
-            it = ps_t.tile([P, SLOTS, P], BF16, tag="t")
-            its[b] = it
-            for j in range(SLOTS):
-                nc.tensor.transpose(it[:, j, :], infl(b)[:, j * SPLATS : (j + 1) * SPLATS], ident_b[:])
+        def t_i(b, j0, j1):
+            if j0 == 0:
+                if b == 0:
+                    it = ps_f.tile([P, SLOTS, P], BF16, tag="f_ps")
+                else:
+                    it = ps_t.tile([P, SLOTS, P], BF16, tag="t")
+                its[b] = it
+            it = its[b]
+            for j in range(j0, j1):
+                nc.tensor.transpose(it[:, j, :], i_sb[:, b, j * SPLATS : (j + 1) * SPLATS], ident_b[:])
 
         def c_x(q, s0, s1):
             if q % 2 == 0 and s0 == 0:
@@ -179,16 +173,19 @@ def tile_splatinformationflow_pb_t_kernel(
             f_ps = ps_f.tile([P, FEAT], F32, tag="f_ps")
             fs[n] = f_ps
             nc.tensor.matmul(
-                out=f_ps[:], lhsT=infl_t[n // SLOTS][:, n % SLOTS, :], rhs=dec(n // SLOTS), start=True, stop=True
+                out=f_ps[:], lhsT=infl_t[n // SLOTS][:, n % SLOTS, :], rhs=d_sb[:, n // SLOTS, :], start=True, stop=True
             )
 
         def add_bias(n):
-            z = zpool.tile([P, FEAT], F32)
-            zs[n] = z
-            nc.vector.tensor_tensor(out=z[:], in0=gs[n][:], in1=bias[:], op=ADD)
+            if n % RUN == 0:
+                zt = zpool.tile([P, RUN, FEAT], F32)
+                z_tiles[n // RUN] = zt
+            zs[n] = z_tiles[n // RUN][:, n % RUN, :]
+            nc.vector.tensor_tensor(out=zs[n], in0=gs[n][:], in1=bias[:], op=ADD)
 
-        def sigmoid(n):
-            nc.scalar.activation(out=zs[n][:], in_=zs[n][:], func=SIGMOID)
+        def sigmoid(r):
+            z = z_tiles[r][:].rearrange("p c d -> p (c d)")
+            nc.scalar.activation(out=z, in_=z, func=SIGMOID)
 
         def by_pool(n):
             return (n % 16 in POOL_TILES and n < 56) or n in POOL_TAIL
@@ -209,7 +206,7 @@ def tile_splatinformationflow_pb_t_kernel(
                     cs = slice(i * w, (i + 1) * w)
                     nc.gpsimd.tensor_tensor(out=o_sbs[g][:, c, cs], in0=f_sbs[n][:, cs], in1=zs[n][:, cs], op=MULT)
             else:
-                nc.vector.tensor_tensor(out=o_sbs[g][:, c, :], in0=fs[n][:], in1=zs[n][:], op=MULT)
+                nc.vector.tensor_tensor(out=o_sbs[g][:, c, :], in0=fs[n][:], in1=zs[n], op=MULT)
 
         def bias_copy():
             nc.vector.tensor_copy(out=bias[:], in_=fs["bias"][:])
@@ -226,31 +223,54 @@ def tile_splatinformationflow_pb_t_kernel(
         def at(when, call, *args):
             calls.append((when, call, args))
 
-        at(-11.5, w_copy, nc.scalar.copy, 384, 512)
-        at(-11.5, w_copy, nc.vector.tensor_copy, 0, 256)
-        at(-11.5, w_copy, nc.vector.tensor_copy, 256, 384)
-        at(-7, w_quantise, 0, 256)
-        at(-5.9, w_quantise, 256, 512)
-        at(-7.5, bias_rows)
-        at(-6.5, bias_copy)
+        bias_rows()
+        w_copy(nc.scalar.copy, 384, 512)
+        w_copy(nc.vector.tensor_copy, 0, 256)
+        w_copy(nc.vector.tensor_copy, 256, 384)
         for s in range(2):
-            at(-11.4 + s * 0.1, t_x, 0, s, s + 1)
-            at(-10 + s * 0.1, c_x, 0, s, s + 1)
-        at(-6.45 + -2, quantise, 0, 0, 2)
-        at(-6.45 + 2, quantise, 0, 2, 2)
-        for q in range(1, N_PAIRS):
-            at(2 * (q - q % 1) - 11.4 + 0.01 * (q % 1), t_x, q, 0, 2)
-            at(2 * q - 10, c_x, q, 0, 2)
+            t_x(0, s, s + 1)
+            c_x(0, s, s + 1)
+        t_x(1, 0, 2)
+        w_quantise(0, 256)
+        w_quantise(256, 512)
+        quantise(0, 0, 1)
+        c_x(1, 0, 2)
+        t_i(0, 0, SLOTS)
+        t_x(2, 0, 2)
+        bias_copy()
+        quantise(0, 1, 1)
+        mx(0)
+        mx(1)
+        c_i(0)
+        add_bias(0)
+        t_x(3, 0, 2)
+        quantise(0, 2, 2)
+        mx(2)
+        c_x(2, 0, 2)
+        sigmoid(0)
+        plain(0)
+        add_bias(1)
+        mx(3)
+        plain(1)
+        c_x(3, 0, 2)
+        for q in range(4, N_PAIRS):
+            at(2 * (q - q % 1) - 11.4 + 0.01 * (q % 1) + (0 if q == 4 else 0), t_x, q, 0, 2)
+            at(2 * q - 10 + (2 if q == 4 else 0), c_x, q, 0, 2)
         for g in range(1, N_TILES // 4):
-            at(4 * g - 6.45, quantise, g, 0, 4)
-        for b in range(BATCH):
-            at(8 * b - 8.8 + (0 if b == 0 else 0), t_i, b)
-            at(8 * b - 7 + (0 if b == 0 else 0), c_i, b)
+            at(4 * g - 6.45 + (2.6 if g == 1 else 0), quantise, g, 0, 4)
+        for b in range(1, BATCH):
+            for j in range(0, SLOTS, 8):
+                at(8 * b - 7.8 + j * 0.25, t_i, b, j, j + 8)
+            at(8 * b - 7, c_i, b)
         for n in range(N_TILES):
-            at(n - 3.5, mx, n)
-            at(n - 1.4, plain, n)
-            at(n - 2.3, add_bias, n)
-            at(n - 0.4, sigmoid, n)
+            if n > 3:
+                at(n - 3.5, mx, n)
+            if n > 1:
+                at(n - 1.4, plain, n)
+            if n > 1:
+                at(n - 2.3, add_bias, n)
+            if n % RUN == 0 and n > 0:
+                at(n - 0.4 - (1 if n < 2 else 0), sigmoid, n // RUN)
             if by_pool(n):
                 at(n - 0.1, flow_copy, n)
             at(n + (0 if by_pool(n) else 0), product, n)

@@ -39,7 +39,7 @@ def tile_splatinformationflow_pb_t_kernel(
         ctx.enter_context(tc.manual_schedule())
         const = ctx.enter_context(tc.tile_pool(name="const", bufs=1))
         stage = ctx.enter_context(tc.tile_pool(name="stage", bufs=3))
-        zpool = ctx.enter_context(tc.tile_pool(name="zpool", bufs=6))
+        zpool = ctx.enter_context(tc.tile_pool(name="zpool", bufs=8))
         fpool = ctx.enter_context(tc.tile_pool(name="fpool", bufs=3))
         opool = ctx.enter_context(tc.tile_pool(name="opool", bufs=6))
         ps_t = ctx.enter_context(tc.psum_pool(name="ps_t", bufs=2))
@@ -188,7 +188,7 @@ def tile_splatinformationflow_pb_t_kernel(
             nc.scalar.activation(out=z, in_=z, func=SIGMOID)
 
         def by_pool(n):
-            return (n % 16 in POOL_TILES and n < 56) or n in POOL_TAIL
+            return n % 16 in (3, 5, 7, 11, 15) and n < 56 or n == 58
 
         def flow_copy(n):
             f_sb = fpool.tile([P, FEAT], F32)
@@ -254,23 +254,24 @@ def tile_splatinformationflow_pb_t_kernel(
         plain(1)
         c_x(3, 0, 2)
         for q in range(4, N_PAIRS):
-            at(2 * (q - q % 1) - 11.4 + 0.01 * (q % 1) + (0 if q == 4 else 0), t_x, q, 0, 2)
+            for s in range(2):
+                at(2 * q + 0.001 * s - 11.4 + (0 if q == 4 else 0), t_x, q, s, s + 1)
             at(2 * q - 10 + (2 if q == 4 else 0), c_x, q, 0, 2)
         for g in range(1, N_TILES // 4):
-            at(4 * g - 6.45 + (2.6 if g == 1 else 0), quantise, g, 0, 4)
+            at(4 * g - 6.45 + (2 if g == 1 else 0), quantise, g, 0, 4)
         for b in range(1, BATCH):
             for j in range(0, SLOTS, 8):
-                at(8 * b - 7.8 + j * 0.25, t_i, b, j, j + 8)
-            at(8 * b - 7, c_i, b)
+                at(8 * b - 7.3 + j * 0.25, t_i, b, j, j + 8)
+            at(8 * b - 6, c_i, b)
         for n in range(N_TILES):
             if n > 3:
-                at(n - 3.5, mx, n)
+                at(n - 3.5 + (0 if n % 2 else 0), mx, n)
             if n > 1:
-                at(n - 1.4, plain, n)
+                at(n - 1.9 + (0 if n % 2 else 0), plain, n)
             if n > 1:
-                at(n - 2.3, add_bias, n)
+                at(n - 2.5, add_bias, n)
             if n % RUN == 0 and n > 0:
-                at(n - 0.4 - (1 if n < 2 else 0), sigmoid, n // RUN)
+                at(n - 1.5 - (1.5 if n < 2 else 0), sigmoid, n // RUN)
             if by_pool(n):
                 at(n - 0.1, flow_copy, n)
             at(n + (0 if by_pool(n) else 0), product, n)

@@ -124,7 +124,7 @@ def tile_splatinformationflow_pb_t_kernel(
                 if b == 0:
                     it = ps_f.tile([P, SLOTS, P], BF16, tag="f_ps")
                 else:
-                    it = ps_t.tile([P, SLOTS, P], BF16, tag="t")
+                    it = ps_f.tile([P, SLOTS, P], BF16, tag="f_ps")
                 its[b] = it
             it = its[b]
             for j in range(j0, j1):
@@ -255,19 +255,19 @@ def tile_splatinformationflow_pb_t_kernel(
         c_x(3, 0, 2)
         for q in range(4, N_PAIRS):
             for s in range(2):
-                at(2 * q + 0.001 * s - 11.4 + (0 if q == 4 else 0), t_x, q, s, s + 1)
+                at(2 * q + 0.001 * s - 11.45 + (0 if q == 4 else 0), t_x, q, s, s + 1)
             at(2 * q - 10 + (2 if q == 4 else 0), c_x, q, 0, 2)
         for g in range(1, N_TILES // 4):
             at(4 * g - 6.45 + (2 if g == 1 else 0), quantise, g, 0, 4)
         for b in range(1, BATCH):
             for j in range(0, SLOTS, 8):
-                at(8 * b - 7.3 + j * 0.25, t_i, b, j, j + 8)
-            at(8 * b - 6, c_i, b)
+                at(8 * b - 6.44 + j * 0.25, t_i, b, j, j + 8)
+            at(8 * b - 5.54, c_i, b)
         for n in range(N_TILES):
             if n > 3:
                 at(n - 3.5 + (0 if n % 2 else 0), mx, n)
             if n > 1:
-                at(n - 1.9 + (0 if n % 2 else 0), plain, n)
+                at(n - 1.4 + (0 if n % 2 else 0), plain, n)
             if n > 1:
                 at(n - 2.5, add_bias, n)
             if n % RUN == 0 and n > 0:
@@ -276,7 +276,7 @@ def tile_splatinformationflow_pb_t_kernel(
                 at(n - 0.1, flow_copy, n)
             at(n + (0 if by_pool(n) else 0), product, n)
             if n >= N_TILES - STORE:
-                at(n + 0.05, store, n, n + 1)
+                at(n + 0.05 + (0 if n == 60 else 0), store, n, n + 1)
             elif n % 2 == 1:
                 at(n + 1.05, store, n - 1, n + 1)
         for when, call, args in sorted(calls, key=lambda c: c[0]):

@@ -54,15 +54,15 @@ def tile_splatinformationflow_pb_t_kernel(
         w_codes = const.tile([P, FEAT], U32, align_bytes=64)
         w_scales = const.tile([P, FEAT], U8, align_bytes=64)
         b_row = const.tile([P, FEAT], BF16)
-        ones = const.tile([P, P], BF16)
+        ones = const.tile([P, FEAT], BF16)
         bias = const.tile([P, FEAT], F32)
         ident_f = const.tile([P, P], F32)
         ident_b = const.tile([P, P], BF16)
         warm = const.tile([P, 1], F32)
 
+        nc.vector.memset(ones[:], 1.0)
         nc.vector.memset(warm[:], 0.0)
         nc.vector.memset(b_row[:], 0.0)
-        nc.vector.memset(ones[:], 1.0)
         nc.scalar.activation(out=warm[:], in_=warm[:], func=SIGMOID)
         make_identity(nc, ident_f[:])
         make_identity(nc, ident_b[:])
@@ -103,10 +103,14 @@ def tile_splatinformationflow_pb_t_kernel(
                 in_=w_grp[:, c0:c1, :].rearrange("p n t -> p (n t)"),
             )
 
+        def warm_up(count):
+            for i in range(count):
+                nc.tensor.matmul(out=dummy[:], lhsT=ones[:, 0:P], rhs=ones[:], start=True, stop=True)
+
         def bias_rows():
             b_ps = ps_f.tile([P, FEAT], F32, tag="f_ps")
             fs["bias"] = b_ps
-            nc.tensor.matmul(out=b_ps[:], lhsT=ones[:], rhs=b_row[:], start=True, stop=True)
+            nc.tensor.matmul(out=b_ps[:], lhsT=ones[:, 0:P], rhs=b_row[:], start=True, stop=True)
 
         def t_x(q, s0, s1):
             words = x_sb[q // 4][:].bitcast(F32)
@@ -157,7 +161,7 @@ def tile_splatinformationflow_pb_t_kernel(
 
         def mx(n):
             cols = slice((n % 4) * P, (n % 4 + 1) * P)
-            g_ps = ps_g.tile([P, FEAT], F32)
+            g_ps = ps_g.tile([P, FEAT], F32, name="g_ps")
             gs[n] = g_ps
             nc.tensor.matmul_mx(
                 out=g_ps[:],
@@ -223,6 +227,8 @@ def tile_splatinformationflow_pb_t_kernel(
         def at(when, call, *args):
             calls.append((when, call, args))
 
+        dummy = ps_g.tile([P, FEAT], F32, name="g_ps")
+        warm_up(6)
         bias_rows()
         w_copy(nc.scalar.copy, 384, 512)
         w_copy(nc.vector.tensor_copy, 0, 256)
@@ -230,16 +236,17 @@ def tile_splatinformationflow_pb_t_kernel(
         for s in range(2):
             t_x(0, s, s + 1)
             c_x(0, s, s + 1)
+        warm_up(1)
         t_x(1, 0, 2)
         w_quantise(0, 256)
         w_quantise(256, 512)
         quantise(0, 0, 1)
         c_x(1, 0, 2)
         t_i(0, 0, SLOTS)
-        t_x(2, 0, 2)
+        mx(0)
         bias_copy()
         quantise(0, 1, 1)
-        mx(0)
+        t_x(2, 0, 2)
         mx(1)
         c_i(0)
         add_bias(0)

@@ -22,7 +22,7 @@ FLOPS = 2 * BATCH * TOKENS * FEAT * FEAT + 2 * BATCH * TOKENS * SPLATS * FEAT
 
 POOL_TILES = (3, 7, 11, 15, 5, 13)
 POOL_TAIL = (56, 58)
-CHUNKS = 2
+CHUNKS = 1
 RUN = 1
 
 
@@ -142,10 +142,10 @@ def tile_splatinformationflow_pb_t_kernel(
             a = 2 * (q % 2)
             nc.scalar.copy(out=dst[:, a + s0 : a + s1], in_=xts[q][:, s0:s1].rearrange("p s u r -> p s r u"))
 
-        def c_i(b):
+        def c_i(b, copy=nc.scalar.copy):
             i_t = stage.tile([P, SLOTS, P], BF16, bufs=2)
             infl_t[b] = i_t
-            nc.scalar.copy(out=i_t[:], in_=its[b][:])
+            copy(out=i_t[:], in_=its[b][:])
 
         def quantise(g, first, count):
             if first == 0:
@@ -243,21 +243,21 @@ def tile_splatinformationflow_pb_t_kernel(
         quantise(0, 0, 1)
         c_x(1, 0, 2)
         t_i(0, 0, SLOTS)
-        mx(0)
+        t_x(2, 0, 2)
         bias_copy()
         quantise(0, 1, 1)
-        t_x(2, 0, 2)
+        mx(0)
         mx(1)
         c_i(0)
+        quantise(0, 2, 2)
+        c_x(2, 0, 2)
         add_bias(0)
         t_x(3, 0, 2)
-        quantise(0, 2, 2)
         mx(2)
-        c_x(2, 0, 2)
-        sigmoid(0)
+        mx(3)
         plain(0)
         add_bias(1)
-        mx(3)
+        sigmoid(0)
         plain(1)
         c_x(3, 0, 2)
         for q in range(4, N_PAIRS):
@@ -272,17 +272,17 @@ def tile_splatinformationflow_pb_t_kernel(
             at(8 * b - 5.54, c_i, b)
         for n in range(N_TILES):
             if n > 3:
-                at(n - 3.5 + (0 if n % 2 else 0), mx, n)
+                at(n - 3.5 - (0 if n > 58 else 0) + (0 if n % 2 else 0), mx, n)
             if n > 1:
                 at(n - 1.4 + (0 if n % 2 else 0), plain, n)
             if n > 1:
-                at(n - 2.5, add_bias, n)
+                at(n - 2.5 - (0 if n > 58 else 0), add_bias, n)
             if n % RUN == 0 and n > 0:
-                at(n - 1.5 - (1.5 if n < 2 else 0), sigmoid, n // RUN)
+                at(n - 1.5 - (0 if n > 58 else 0) - (1.5 if n < 2 else 0), sigmoid, n // RUN)
             if by_pool(n):
                 at(n - 0.1, flow_copy, n)
             at(n + (0 if by_pool(n) else 0), product, n)
-            if n >= N_TILES - STORE:
+            if n >= N_TILES - 4:
                 at(n + 0.05 + (0 if n == 60 else 0), store, n, n + 1)
             elif n % 2 == 1:
                 at(n + 1.05, store, n - 1, n + 1)

from contextlib import ExitStack

import concourse.mybir as mybir
from concourse.masks import make_identity

F32 = mybir.dt.float32
BF16 = mybir.dt.bfloat16
U32 = mybir.dt.uint32
U8 = mybir.dt.uint8
FP8X4 = mybir.dt.float8_e4m3fn_x4
ADD = mybir.AluOpType.add
MULT = mybir.AluOpType.mult
SIGMOID = mybir.ActivationFunctionType.Sigmoid

P = 128
BATCH, TOKENS, FEAT, SPLATS = 8, 1024, 512, 128
SLOTS = TOKENS // P
N_TILES = BATCH * SLOTS
N_PAIRS = N_TILES // 2
STORE = 4
FLOPS = 2 * BATCH * TOKENS * FEAT * FEAT + 2 * BATCH * TOKENS * SPLATS * FEAT

POOL_TILES = (3, 7, 11, 15, 5, 13)
POOL_TAIL = (56, 58)
CHUNKS = 1
RUN = 1


def tile_splatinformationflow_pb_t_kernel(
    tc, token_embeddings, splat_influences, decoded, gate_W, gate_b, out
):
    nc = tc.nc
    x_dram = token_embeddings.rearrange("b (p j) k -> b p (j k)", j=SLOTS)
    i_dram = splat_influences.rearrange("b (p j) s -> p b (j s)", j=SLOTS)
    d_dram = decoded.rearrange("b s d -> s b d")
    o_dram = out.rearrange("b (p j) d -> b p (j d)", j=SLOTS)

    with ExitStack() as ctx:
        ctx.enter_context(tc.manual_schedule())
        const = ctx.enter_context(tc.tile_pool(name="const", bufs=1))
        stage = ctx.enter_context(tc.tile_pool(name="stage", bufs=3))
        zpool = ctx.enter_context(tc.tile_pool(name="zpool", bufs=8))
        fpool = ctx.enter_context(tc.tile_pool(name="fpool", bufs=3))
        opool = ctx.enter_context(tc.tile_pool(name="opool", bufs=6))
        ps_t = ctx.enter_context(tc.psum_pool(name="ps_t", bufs=2))
        ps_g = ctx.enter_context(tc.psum_pool(name="ps_g", bufs=3))
        ps_f = ctx.enter_context(tc.psum_pool(name="ps_f", bufs=3))

        x_sb = [const.tile([P, SLOTS * FEAT], BF16, name="x%d" % b) for b in range(BATCH)]
        i_sb = const.tile([P, BATCH, SLOTS * SPLATS], BF16)
        d_sb = const.tile([P, BATCH, FEAT], BF16)
        w_raw = const.tile([P, 4, FEAT], BF16)
        w_grp = const.tile([P, FEAT, 4], BF16, align_bytes=64)
        w_codes = const.tile([P, FEAT], U32, align_bytes=64)
        w_scales = const.tile([P, FEAT], U8, align_bytes=64)
        b_row = const.tile([P, FEAT], BF16)
        ones = const.tile([P, FEAT], BF16)
        bias = const.tile([P, FEAT], F32)
        ident_f = const.tile([P, P], F32)
        ident_b = const.tile([P, P], BF16)
        warm = const.tile([P, 1], F32)

        nc.vector.memset(ones[:], 1.0)
        nc.vector.memset(warm[:], 0.0)
        nc.vector.memset(b_row[:], 0.0)
        nc.scalar.activation(out=warm[:], in_=warm[:], func=SIGMOID)
        make_identity(nc, ident_f[:])
        make_identity(nc, ident_b[:])

        def load_x(b, j0, j1):
            cols = slice(j0 * FEAT, j1 * FEAT)
            nc.sync.dma_start(out=x_sb[b][:, cols], in_=x_dram[b][:, cols])

        nc.sync.dma_start(out=w_raw[:], in_=gate_W.rearrange("(q t) n -> q t n", t=4))
        nc.sync.dma_start(out=b_row[0:1, :], in_=gate_b.rearrange("(o n) -> o n", o=1))
        load_x(0, 0, 1)
        load_x(0, 1, 2)
        load_x(0, 2, 4)
        nc.sync.dma_start(out=i_sb[:, 0:1, :], in_=i_dram[:, 0:1, :])
        load_x(0, 4, 6)
        nc.sync.dma_start(out=d_sb[:, 0:1, :], in_=d_dram[:, 0:1, :])
        load_x(0, 6, 8)
        load_x(1, 0, 4)
        load_x(1, 4, 8)
        nc.sync.dma_start(out=i_sb[:, 1:2, :], in_=i_dram[:, 1:2, :])
        nc.sync.dma_start(out=d_sb[:, 1:8, :], in_=d_dram[:, 1:8, :])
        nc.sync.dma_start(out=i_sb[:, 2:4, :], in_=i_dram[:, 2:4, :])
        load_x(2, 0, 8)
        load_x(3, 0, 8)
        nc.sync.dma_start(out=i_sb[:, 4:8, :], in_=i_dram[:, 4:8, :])
        for b in range(4, BATCH):
            load_x(b, 0, 8)

        xts, its, grps, codes, planes, infl_t, gs, fs, f_sbs, zs, z_tiles, o_sbs = {}, {}, {}, {}, {}, {}, {}, {}, {}, {}, {}, {}

        def w_copy(copy, c0, c1):
            copy(out=w_grp[:, c0:c1, :], in_=w_raw[:, :, c0:c1].rearrange("p t n -> p n t"))

        def w_quantise(c0, c1):
            nc.vector.quantize_mx(
                out=w_codes[:, c0:c1].bitcast(FP8X4),
                scales=w_scales[:, c0:c1],
                in_=w_grp[:, c0:c1, :].rearrange("p n t -> p (n t)"),
            )

        def warm_up(count):
            for i in range(count):
                nc.tensor.matmul(out=dummy[:], lhsT=ones[:, 0:P], rhs=ones[:], start=True, stop=True)

        def bias_rows():
            b_ps = ps_f.tile([P, FEAT], F32, tag="f_ps")
            fs["bias"] = b_ps
            nc.tensor.matmul(out=b_ps[:], lhsT=ones[:, 0:P], rhs=b_row[:], start=True, stop=True)

        def t_x(q, s0, s1):
            words = x_sb[q // 4][:].bitcast(F32)
            if s0 == 0:
                xt = ps_t.tile([P, 2, 2, P], F32, tag="t")
                xts[q] = xt
            xt = xts[q]
            for s in range(s0, s1):
                for u in range(2):
                    w0 = (2 * (q % 4) + s) * (FEAT // 2)
                    nc.tensor.transpose(xt[:, s, u, :], words[:, w0 + u : w0 + 2 * P : 2], ident_f[:])

        def t_i(b, j0, j1):
            if j0 == 0:
                if b == 0:
                    it = ps_f.tile([P, SLOTS, P], BF16, tag="f_ps")
                else:
                    it = ps_f.tile([P, SLOTS, P], BF16, tag="f_ps")
                its[b] = it
            it = its[b]
            for j in range(j0, j1):
                nc.tensor.transpose(it[:, j, :], i_sb[:, b, j * SPLATS : (j + 1) * SPLATS], ident_b[:])

        def c_x(q, s0, s1):
            if q % 2 == 0 and s0 == 0:
                grp = stage.tile([P, 4 * P * 4], BF16, align_bytes=64)
                grps[q // 2] = grp
            dst = grps[q // 2][:].bitcast(F32).rearrange("p (s r u) -> p s r u", s=4, u=2)
            a = 2 * (q % 2)
            nc.scalar.copy(out=dst[:, a + s0 : a + s1], in_=xts[q][:, s0:s1].rearrange("p s u r -> p s r u"))

        def c_i(b, copy=nc.scalar.copy):
            i_t = stage.tile([P, SLOTS, P], BF16, bufs=2)
            infl_t[b] = i_t
            copy(out=i_t[:], in_=its[b][:])

        def quantise(g, first, count):
            if first == 0:
                cod = stage.tile([P, 4 * P], U32, align_bytes=64)
                pla = stage.tile([P, 4 * P], U8, align_bytes=64)
                codes[g], planes[g] = cod, pla
            cols = slice(first * P, (first + count) * P)
            nc.vector.quantize_mx(
                out=codes[g][:, cols].bitcast(FP8X4),
                scales=planes[g][:, cols],
                in_=grps[g][:, 4 * first * P : 4 * (first + count) * P],
            )

        def mx(n):
            cols = slice((n % 4) * P, (n % 4 + 1) * P)
            g_ps = ps_g.tile([P, FEAT], F32, name="g_ps")
            gs[n] = g_ps
            nc.tensor.matmul_mx(
                out=g_ps[:],
                lhsT=codes[n // 4][:, cols].bitcast(FP8X4),
                lhsT_scale=planes[n // 4][:, cols],
                rhs=w_codes[:].bitcast(FP8X4),
                rhs_scale=w_scales[:],
                start=True,
                stop=True,
            )

        def plain(n):
            f_ps = ps_f.tile([P, FEAT], F32, tag="f_ps")
            fs[n] = f_ps
            nc.tensor.matmul(
                out=f_ps[:], lhsT=infl_t[n // SLOTS][:, n % SLOTS, :], rhs=d_sb[:, n // SLOTS, :], start=True, stop=True
            )

        def add_bias(n):
            if n % RUN == 0:
                zt = zpool.tile([P, RUN, FEAT], F32)
                z_tiles[n // RUN] = zt
            zs[n] = z_tiles[n // RUN][:, n % RUN, :]
            nc.vector.tensor_tensor(out=zs[n], in0=gs[n][:], in1=bias[:], op=ADD)

        def sigmoid(r):
            z = z_tiles[r][:].rearrange("p c d -> p (c d)")
            nc.scalar.activation(out=z, in_=z, func=SIGMOID)

        def by_pool(n):
            return n % 16 in (3, 5, 7, 11, 15) and n < 56 or n == 58

        def flow_copy(n):
            f_sb = fpool.tile([P, FEAT], F32)
            f_sbs[n] = f_sb
            nc.scalar.copy(out=f_sb[:], in_=fs[n][:])

        def product(n):
            g, c = n // STORE, n % STORE
            if c == 0:
                o = opool.tile([P, STORE, FEAT], F32)
                o_sbs[g] = o
            if by_pool(n):
                w = FEAT // CHUNKS
                for i in range(CHUNKS):
                    cs = slice(i * w, (i + 1) * w)
                    nc.gpsimd.tensor_tensor(out=o_sbs[g][:, c, cs], in0=f_sbs[n][:, cs], in1=zs[n][:, cs], op=MULT)
            else:
                nc.vector.tensor_tensor(out=o_sbs[g][:, c, :], in0=fs[n][:], in1=zs[n], op=MULT)

        def bias_copy():
            nc.vector.tensor_copy(out=bias[:], in_=fs["bias"][:])

        def store(n0, n1):
            b, g = n0 // SLOTS, n0 // STORE
            nc.sync.dma_start(
                out=o_dram[b][:, (n0 % SLOTS) * FEAT : (n0 % SLOTS + n1 - n0) * FEAT],
                in_=o_sbs[g][:, n0 % STORE : n0 % STORE + n1 - n0, :].rearrange("p c d -> p (c d)"),
            )

        calls = []

        def at(when, call, *args):
            calls.append((when, call, args))

        dummy = ps_g.tile([P, FEAT], F32, name="g_ps")
        warm_up(6)
        bias_rows()
        w_copy(nc.scalar.copy, 384, 512)
        w_copy(nc.vector.tensor_copy, 0, 256)
        w_copy(nc.vector.tensor_copy, 256, 384)
        for s in range(2):
            t_x(0, s, s + 1)
            c_x(0, s, s + 1)
        warm_up(1)
        t_x(1, 0, 2)
        w_quantise(0, 256)
        w_quantise(256, 512)
        quantise(0, 0, 1)
        c_x(1, 0, 2)
        t_i(0, 0, SLOTS)
        t_x(2, 0, 2)
        bias_copy()
        quantise(0, 1, 1)
        mx(0)
        mx(1)
        c_i(0)
        quantise(0, 2, 2)
        c_x(2, 0, 2)
        add_bias(0)
        t_x(3, 0, 2)
        mx(2)
        mx(3)
        plain(0)
        add_bias(1)
        sigmoid(0)
        plain(1)
        c_x(3, 0, 2)
        for q in range(4, N_PAIRS):
            for s in range(2):
                at(2 * q + 0.001 * s - 11.45 + (0 if q == 4 else 0), t_x, q, s, s + 1)
            at(2 * q - 10 + (2 if q == 4 else 0), c_x, q, 0, 2)
        for g in range(1, N_TILES // 4):
            at(4 * g - 6.45 + (2 if g == 1 else 0), quantise, g, 0, 4)
        for b in range(1, BATCH):
            for j in range(0, SLOTS, 8):
                at(8 * b - 6.44 + j * 0.25, t_i, b, j, j + 8)
            at(8 * b - 5.54, c_i, b)
        for n in range(N_TILES):
            if n > 3:
                at(n - 3.5 - (0 if n > 58 else 0) + (0 if n % 2 else 0), mx, n)
            if n > 1:
                at(n - 1.4 + (0 if n % 2 else 0), plain, n)
            if n > 1:
                at(n - 2.5 - (0 if n > 58 else 0), add_bias, n)
            if n % RUN == 0 and n > 0:
                at(n - 1.5 - (0 if n > 58 else 0) - (1.5 if n < 2 else 0), sigmoid, n // RUN)
            if by_pool(n):
                at(n - 0.1, flow_copy, n)
            at(n + (0 if by_pool(n) else 0), product, n)
            if n >= N_TILES - 4:
                at(n + 0.05 + (0 if n == 60 else 0), store, n, n + 1)
            elif n % 2 == 1:
                at(n + 1.05, store, n - 1, n + 1)
        for when, call, args in sorted(calls, key=lambda c: c[0]):
            call(*args)
